import numpy as np
import ml_dtypes


BF16 = ml_dtypes.bfloat16


def bf(x):
    return np.asarray(x, np.float32).astype(BF16)


def f64(x):
    return np.asarray(x).astype(np.float64)


E2M1 = np.array([0.0, 0.5, 1.0, 1.5, 2.0, 3.0, 4.0, 6.0, -0.0, -0.5, -1.0, -1.5, -2.0, -3.0, -4.0, -6.0])


def pack_weight(w, fmt):
    k, n = w.shape
    w = f64(bf(w)).reshape(k // 32, 32, n)
    amax = np.abs(w).max(1)
    if fmt == "e4m3":
        byte = np.frexp(amax)[1] - 1 + 127 - 7
    else:
        mant, ex = np.frexp(amax / 6.0)
        byte = np.where(mant > 0.5, ex, ex - 1) + 127
    byte = np.clip(np.where(amax > 0, byte, 1), 1, 254)
    scaled = (w * np.exp2(127.0 - byte)[:, None, :]).reshape(k, n).astype(np.float32)
    by_word = np.ascontiguousarray(scaled.reshape(k // 512, 128, 4, n).transpose(0, 1, 3, 2))
    if fmt == "e4m3":
        words = by_word.astype(ml_dtypes.float8_e4m3fn).view(np.uint8)
    else:
        c = by_word.astype(ml_dtypes.float4_e2m1fn).view(np.uint8) & 0xF
        words = c[..., 0::2] | (c[..., 1::2] << 4)
    return np.ascontiguousarray(words), np.ascontiguousarray(byte.astype(np.uint8).reshape(k // 512, 16, n))


def unpack_weight(words, scales, fmt):
    g, p, n, _ = words.shape
    if fmt == "e4m3":
        vals = np.ascontiguousarray(words).view(ml_dtypes.float8_e4m3fn).astype(np.float64)
    else:
        nib = np.empty((g, p, n, 4), np.uint8)
        nib[..., 0::2] = words & 0xF
        nib[..., 1::2] = words >> 4
        vals = E2M1[nib]
    vals = vals * np.repeat(np.exp2(scales.astype(np.float64) - 127.0), 8, axis=1)[..., None]
    return vals.transpose(0, 1, 3, 2).reshape(g * 512, n)

def pack4(w):
    words, scales = pack_weight(w, "e2m1")
    return words.reshape(words.shape[0], 128, -1), scales


def unpack4(words, scales):
    return unpack_weight(words.reshape(words.shape[0], 128, -1, 2), scales, "e2m1")


def kspread(k):
    return np.exp2(np.repeat(np.random.randint(-6, 7, k // 32), 32).astype(np.float64))


G1, G2, B, DIM, K, N = 8, 8, 48, 2, 8192, 512


def sigmoid(v):
    return 1.0 / (1.0 + np.exp(-v))


def setup_inputs():
    s = kspread(K)
    a = 1.5 / np.sqrt(K)
    r = np.random.standard_normal
    x = r((G1, G2, B, K)) * s
    x_words, x_scales = pack4(x.reshape(G1 * G2 * B, K).T)
    wf = bf(r((DIM, K, N)) * a)
    uf = bf(r((DIM, DIM, N)) * 0.5)
    biasf = bf(r((DIM, N)) * 0.5)
    wi = bf(r((K, N)) * a)
    ui = bf(r((DIM, N)) * 0.5)
    biasi = bf(r(N) * 0.5)
    wo_words, wo_scales = pack4(r((K, N)) * a / s[:, None])
    uo = bf(r((DIM, N)) * 0.5)
    biaso = bf(r(N) * 0.5)
    wc_words, wc_scales = pack4(r((K, N)) * a / s[:, None])
    uc = bf(r((DIM, N)) * 0.5)
    biasc = bf(r(N) * 0.5)
    return {
        "x_words": x_words,
        "x_scales": x_scales,
        "wf": wf,
        "uf": uf,
        "biasf": biasf,
        "wi": wi,
        "ui": ui,
        "biasi": biasi,
        "wo_words": wo_words,
        "wo_scales": wo_scales,
        "uo": uo,
        "biaso": biaso,
        "wc_words": wc_words,
        "wc_scales": wc_scales,
        "uc": uc,
        "biasc": biasc,
    }


def reference(x_words, x_scales, wf, uf, biasf, wi, ui, biasi, wo_words, wo_scales, uo, biaso, wc_words, wc_scales, uc, biasc):
    xq = unpack4(x_words, x_scales).T.reshape(G1, G2, B, K)
    o = sigmoid((xq @ unpack4(wo_words, wo_scales)) + f64(biaso))
    c = sigmoid((xq @ unpack4(wc_words, wc_scales)) + f64(biasc))
    return o * np.tanh(c)

@@ -1,0 +1,187 @@
+from contextlib import ExitStack
+
+import concourse.mybir as mybir
+
+ROWS, K, N = 3072, 8192, 512
+
+F32 = mybir.dt.float32
+BF16 = mybir.dt.bfloat16
+I32 = mybir.dt.int32
+U8 = mybir.dt.uint8
+FP4X4 = mybir.dt.float4_e2m1fn_x4
+ADD = mybir.AluOpType.add
+MULT = mybir.AluOpType.mult
+SIGMOID = mybir.ActivationFunctionType.Sigmoid
+TANH = mybir.ActivationFunctionType.Tanh
+
+P = 128
+PASSES = K // 512
+BLOCK = 1024
+TILES = BLOCK // P
+BLOCKS = ROWS // BLOCK
+TAIL = 4
+WARM = 7
+
+FLOPS = 2 * ROWS * K * (2 * N)
+BYTES = ROWS * K // 2 + ROWS * K // 32 + 2 * (N * K // 2 + N * K // 32) + 2 * 2 * N + 4 * ROWS * N
+
+
+def tile_mdlstm_kernel(
+    tc, x_words, x_scales, wf, uf, biasf, wi, ui, biasi, wo_words, wo_scales, uo, biaso, wc_words, wc_scales, uc, biasc, out
+):
+    nc = tc.nc
+    out_rows = out.rearrange("i j b n -> (i j b) n")
+
+    with ExitStack() as ctx:
+        keep = ctx.enter_context(tc.tile_pool(name="keep", bufs=1))
+        acts = ctx.enter_context(tc.tile_pool(name="acts", bufs=4))
+        psum = ctx.enter_context(tc.psum_pool(name="psum", bufs=1))
+        ctx.enter_context(tc.manual_schedule())
+
+        codes = {}
+        planes = {}
+
+        def new_planes(name, cols, g0, g1):
+            tile = keep.tile([P, g1 - g0, cols], U8, name="%s_planes_%d" % (name, g0), align_bytes=256)
+            nc.vector.memset(tile[:].bitcast(I32), 0)
+            for g in range(g0, g1):
+                planes[name, g] = tile[:, g - g0, :]
+            return tile
+
+        def load_scales(tile, scales, c0, cols, g0, g1):
+            for q in range(4):
+                nc.sync.dma_start(
+                    out=tile[32 * q : 32 * q + 4, :, :].bitcast(I32),
+                    in_=scales[g0:g1, 4 * q : 4 * q + 4, c0 : c0 + cols].rearrange("g r n -> r g n").bitcast(I32),
+                )
+
+        def load_codes(name, words, c0, cols, g0, g1):
+            tile = keep.tile([P, g1 - g0, 2 * cols], U8, name="%s_codes_%d" % (name, g0), align_bytes=256)
+            nc.sync.dma_start(
+                out=tile[:].bitcast(I32),
+                in_=words[g0:g1, :, 2 * c0 : 2 * (c0 + cols)].rearrange("g p n -> p g n").bitcast(I32),
+            )
+            for g in range(g0, g1):
+                codes[name, g] = tile[:, g - g0, :]
+
+        def multiply(acc, w, w0, width, t, g):
+            b, m0 = "x%d" % (t // TILES), P * (t % TILES)
+            nc.tensor.matmul_mx(
+                out=acc,
+                lhsT=codes[b, g][:, 2 * m0 : 2 * (m0 + P)].bitcast(FP4X4),
+                lhsT_scale=planes[b, g][:, m0 : m0 + P],
+                rhs=codes[w, g][:, 2 * w0 : 2 * (w0 + width)].bitcast(FP4X4),
+                rhs_scale=planes[w, g][:, w0 : w0 + width],
+                start=(g == 0),
+                stop=(g == PASSES - 1),
+            )
+
+        def new_bank(i):
+            return psum.tile([P, N], F32, name="bank%d" % i)
+
+        scale_runs = [(0, 2), (2, 6), (6, 11), (11, 16)]
+        tiles0 = {}
+        warm = keep.tile([P, N], BF16)
+        nc.gpsimd.memset(warm[:], 0.0)
+        for g0, g1 in scale_runs:
+            tiles0["x0", g0] = new_planes("x0", BLOCK, g0, g1)
+            tiles0["wo", g0] = new_planes("wo", N, g0, g1)
+        wc_planes = new_planes("wc", N, 0, PASSES)
+        x1_planes = new_planes("x1", BLOCK, 0, PASSES)
+        x2_planes = new_planes("x2", BLOCK, 0, PASSES)
+
+        def x0_wo_codes(g0, g1):
+            load_codes("x0", x_words, 0, BLOCK, g0, g1)
+            load_codes("wo", wo_words, 0, N, g0, g1)
+
+        def x0_wo_scales(g0, g1):
+            load_scales(tiles0["x0", g0], x_scales, 0, BLOCK, g0, g1)
+            load_scales(tiles0["wo", g0], wo_scales, 0, N, g0, g1)
+
+        x0_wo_codes(0, 1)
+        x0_wo_scales(0, 2)
+        x0_wo_codes(1, 2)
+        x0_wo_codes(2, 4)
+        x0_wo_scales(2, 6)
+        x0_wo_codes(4, 8)
+        x0_wo_scales(6, 11)
+        x0_wo_codes(8, 12)
+        x0_wo_scales(11, 16)
+        x0_wo_codes(12, 16)
+
+        bias_o = keep.tile([P, N], BF16)
+        nc.sync.dma_start(out=bias_o[:], in_=biaso.partition_broadcast(P))
+        bias_c = keep.tile([P, N], BF16)
+        nc.sync.dma_start(out=bias_c[:], in_=biasc.partition_broadcast(P))
+
+        load_codes("wc", wc_words, 0, N, 0, 8)
+        load_codes("wc", wc_words, 0, N, 8, 16)
+        load_scales(wc_planes, wc_scales, 0, N, 0, PASSES)
+
+        def load_block(i, x_planes):
+            for g0 in range(0, PASSES, 4):
+                load_codes("x%d" % i, x_words, i * BLOCK, BLOCK, g0, g0 + 4)
+            load_scales(x_planes, x_scales, i * BLOCK, BLOCK, 0, PASSES)
+
+        load_block(1, x1_planes)
+
+        scrap = new_bank(7)
+        for i in range(WARM):
+            nc.tensor.matmul(scrap[:], warm[:, 0:P], warm[:], start=True, stop=True)
+
+        def gate_o(t, acc):
+            o = acts.tile([P, N], F32, name="o", bufs=9)
+            nc.vector.tensor_tensor(out=o[:], in0=acc[:], in1=bias_o[:], op=ADD)
+            nc.scalar.activation(o[:], o[:], SIGMOID)
+            return o
+
+        def finish(t, acc, o):
+            c = acts.tile([P, N], F32, name="c", bufs=4)
+            nc.vector.tensor_tensor(out=c[:], in0=acc[:], in1=bias_c[:], op=ADD)
+            nc.scalar.activation(c[:], c[:], SIGMOID)
+            nc.scalar.activation(c[:], c[:], TANH)
+            nc.vector.tensor_tensor(out=c[:], in0=c[:], in1=o[:], op=MULT)
+            nc.sync.dma_start(out=out_rows[P * t : P * (t + 1), :], in_=c[:])
+
+        banks = [new_bank(t) for t in range(TILES)]
+        for g in range(PASSES - TAIL):
+            for t in range(TILES):
+                multiply(banks[t][:], "wo", 0, N, t, g)
+        o_tiles = []
+        for t in range(TILES):
+            for g in range(PASSES - TAIL, PASSES):
+                multiply(banks[t][:], "wo", 0, N, t, g)
+            o_tiles.append(gate_o(t, banks[t]))
+
+        for t in range(TILES):
+            acc = new_bank(t)
+            for g in range(PASSES):
+                multiply(acc[:], "wc", 0, N, t, g)
+            finish(t, acc, o_tiles[t])
+
+        load_block(2, x2_planes)
+
+        last = BLOCKS * TILES - 1
+        for t in range(TILES, last + 1):
+            acc = new_bank(2 * t % 8)
+            for g in range(PASSES):
+                multiply(acc[:], "wo", 0, N, t, g)
+            o = gate_o(t, acc)
+            if t < last:
+                acc = new_bank((2 * t + 1) % 8)
+                for g in range(PASSES):
+                    multiply(acc[:], "wc", 0, N, t, g)
+                finish(t, acc, o)
+
+        c = acts.tile([P, N], F32, name="c", bufs=4)
+        pieces = [(0, 256), (256, 128), (384, 128)]
+        for i, (n0, width) in enumerate(pieces):
+            acc = new_bank((7 + i) % 8)
+            cols = slice(n0, n0 + width)
+            for g in range(PASSES):
+                multiply(acc[:, 0:width], "wc", n0, width, last, g)
+            nc.vector.tensor_tensor(out=c[:, cols], in0=acc[:, 0:width], in1=bias_c[:, cols], op=ADD)
+            nc.scalar.activation(c[:, cols], c[:, cols], SIGMOID)
+            nc.scalar.activation(c[:, cols], c[:, cols], TANH)
+            nc.vector.tensor_tensor(out=c[:, cols], in0=c[:, cols], in1=o[:, cols], op=MULT)
+            nc.sync.dma_start(out=out_rows[P * last : P * (last + 1), cols], in_=c[:, cols])

@@ -56,19 +56,21 @@ def tile_mdlstm_kernel(
                 )
 
         def load_codes(name, words, c0, cols, g0, g1):
-            tile = keep.tile([P, g1 - g0, 2 * cols], U8, name="%s_codes_%d" % (name, g0), align_bytes=256)
+            tile = keep.tile([P, g1 - g0, 2 * cols], U8, name="%s_codes_%d_%d" % (name, g0, c0), align_bytes=256)
             nc.sync.dma_start(
                 out=tile[:].bitcast(I32),
                 in_=words[g0:g1, :, 2 * c0 : 2 * (c0 + cols)].rearrange("g p n -> p g n").bitcast(I32),
             )
             for g in range(g0, g1):
+                for col in range(c0, c0 + cols, P):
+                    codes[name[0:1], g, col] = tile[:, g - g0, 2 * (col - c0) : 2 * (col - c0 + P)]
                 codes[name, g] = tile[:, g - g0, :]
 
         def multiply(acc, w, w0, width, t, g):
             b, m0 = "x%d" % (t // TILES), P * (t % TILES)
             nc.tensor.matmul_mx(
                 out=acc,
-                lhsT=codes[b, g][:, 2 * m0 : 2 * (m0 + P)].bitcast(FP4X4),
+                lhsT=codes["x", g, P * t].bitcast(FP4X4),
                 lhsT_scale=planes[b, g][:, m0 : m0 + P],
                 rhs=codes[w, g][:, 2 * w0 : 2 * (w0 + width)].bitcast(FP4X4),
                 rhs_scale=planes[w, g][:, w0 : w0 + width],
@@ -85,38 +87,40 @@ def tile_mdlstm_kernel(
         nc.gpsimd.memset(warm[:], 0.0)
         for g0, g1 in scale_runs:
             tiles0["x0", g0] = new_planes("x0", BLOCK, g0, g1)
-            tiles0["wo", g0] = new_planes("wo", N, g0, g1)
-        wc_planes = new_planes("wc", N, 0, PASSES)
+            tiles0["wc", g0] = new_planes("wc", N, g0, g1)
+        wo_planes = new_planes("wo", N, 0, PASSES)
         x1_planes = new_planes("x1", BLOCK, 0, PASSES)
         x2_planes = new_planes("x2", BLOCK, 0, PASSES)
 
-        def x0_wo_codes(g0, g1):
+        def x0_wc_codes(g0, g1):
             load_codes("x0", x_words, 0, BLOCK, g0, g1)
-            load_codes("wo", wo_words, 0, N, g0, g1)
+            load_codes("wc", wc_words, 0, N, g0, g1)
 
-        def x0_wo_scales(g0, g1):
+        def x0_wc_scales(g0, g1):
             load_scales(tiles0["x0", g0], x_scales, 0, BLOCK, g0, g1)
-            load_scales(tiles0["wo", g0], wo_scales, 0, N, g0, g1)
+            load_scales(tiles0["wc", g0], wc_scales, 0, N, g0, g1)
 
-        x0_wo_codes(0, 1)
-        x0_wo_scales(0, 2)
-        x0_wo_codes(1, 2)
-        x0_wo_codes(2, 4)
-        x0_wo_scales(2, 6)
-        x0_wo_codes(4, 8)
-        x0_wo_scales(6, 11)
-        x0_wo_codes(8, 12)
-        x0_wo_scales(11, 16)
-        x0_wo_codes(12, 16)
+        load_codes("x0", x_words, 0, BLOCK // 2, 0, 1)
+        load_codes("wc", wc_words, 0, N, 0, 1)
+        x0_wc_scales(0, 2)
+        load_codes("x0", x_words, BLOCK // 2, BLOCK // 2, 0, 1)
+        x0_wc_codes(1, 2)
+        x0_wc_codes(2, 4)
+        x0_wc_scales(2, 6)
+        x0_wc_codes(4, 8)
+        x0_wc_scales(6, 11)
+        x0_wc_codes(8, 12)
+        x0_wc_scales(11, 16)
+        x0_wc_codes(12, 16)
 
-        bias_o = keep.tile([P, N], BF16)
-        nc.sync.dma_start(out=bias_o[:], in_=biaso.partition_broadcast(P))
         bias_c = keep.tile([P, N], BF16)
         nc.sync.dma_start(out=bias_c[:], in_=biasc.partition_broadcast(P))
+        bias_o = keep.tile([P, N], BF16)
+        nc.sync.dma_start(out=bias_o[:], in_=biaso.partition_broadcast(P))
 
-        load_codes("wc", wc_words, 0, N, 0, 8)
-        load_codes("wc", wc_words, 0, N, 8, 16)
-        load_scales(wc_planes, wc_scales, 0, N, 0, PASSES)
+        load_codes("wo", wo_words, 0, N, 0, 8)
+        load_codes("wo", wo_words, 0, N, 8, 16)
+        load_scales(wo_planes, wo_scales, 0, N, 0, PASSES)
 
         def load_block(i, x_planes):
             for g0 in range(0, PASSES, 4):
@@ -129,35 +133,36 @@ def tile_mdlstm_kernel(
         for i in range(WARM):
             nc.tensor.matmul(scrap[:], warm[:, 0:P], warm[:], start=True, stop=True)
 
-        def gate_o(t, acc):
-            o = acts.tile([P, N], F32, name="o", bufs=9)
-            nc.vector.tensor_tensor(out=o[:], in0=acc[:], in1=bias_o[:], op=ADD)
-            nc.scalar.activation(o[:], o[:], SIGMOID)
-            return o
-
-        def finish(t, acc, o):
-            c = acts.tile([P, N], F32, name="c", bufs=4)
+        def cell(acc):
+            c = acts.tile([P, N], F32, name="c", bufs=9)
             nc.vector.tensor_tensor(out=c[:], in0=acc[:], in1=bias_c[:], op=ADD)
             nc.scalar.activation(c[:], c[:], SIGMOID)
             nc.scalar.activation(c[:], c[:], TANH)
-            nc.vector.tensor_tensor(out=c[:], in0=c[:], in1=o[:], op=MULT)
-            nc.sync.dma_start(out=out_rows[P * t : P * (t + 1), :], in_=c[:])
+            return c
+
+        def finish(t, acc, c, o, n0, width):
+            cols = slice(n0, n0 + width)
+            nc.vector.tensor_tensor(out=o[:, cols], in0=acc[:, 0:width], in1=bias_o[:, cols], op=ADD)
+            nc.scalar.activation(o[:, cols], o[:, cols], SIGMOID)
+            nc.vector.tensor_tensor(out=o[:, cols], in0=o[:, cols], in1=c[:, cols], op=MULT)
+            nc.sync.dma_start(out=out_rows[P * t : P * (t + 1), cols], in_=o[:, cols])
 
         banks = [new_bank(t) for t in range(TILES)]
         for g in range(PASSES - TAIL):
             for t in range(TILES):
-                multiply(banks[t][:], "wo", 0, N, t, g)
-        o_tiles = []
+                multiply(banks[t][:], "wc", 0, N, t, g)
+        cells = []
         for t in range(TILES):
             for g in range(PASSES - TAIL, PASSES):
-                multiply(banks[t][:], "wo", 0, N, t, g)
-            o_tiles.append(gate_o(t, banks[t]))
+                multiply(banks[t][:], "wc", 0, N, t, g)
+            cells.append(cell(banks[t]))
 
         for t in range(TILES):
             acc = new_bank(t)
             for g in range(PASSES):
-                multiply(acc[:], "wc", 0, N, t, g)
-            finish(t, acc, o_tiles[t])
+                multiply(acc[:], "wo", 0, N, t, g)
+            o = acts.tile([P, N], F32, name="o", bufs=4)
+            finish(t, acc, cells[t], o, 0, N)
 
         load_block(2, x2_planes)
 
@@ -165,23 +170,12 @@ def tile_mdlstm_kernel(
         for t in range(TILES, last + 1):
             acc = new_bank(2 * t % 8)
             for g in range(PASSES):
-                multiply(acc[:], "wo", 0, N, t, g)
-            o = gate_o(t, acc)
-            if t < last:
-                acc = new_bank((2 * t + 1) % 8)
+                multiply(acc[:], "wc", 0, N, t, g)
+            c = cell(acc)
+            o = acts.tile([P, N], F32, name="o", bufs=4)
+            pieces = [(0, N)] if t < last else [(0, 256), (256, 128), (384, 128)]
+            for i, (n0, width) in enumerate(pieces):
+                acc = new_bank((2 * t + 1 + i) % 8)
                 for g in range(PASSES):
-                    multiply(acc[:], "wc", 0, N, t, g)
-                finish(t, acc, o)
-
-        c = acts.tile([P, N], F32, name="c", bufs=4)
-        pieces = [(0, 256), (256, 128), (384, 128)]
-        for i, (n0, width) in enumerate(pieces):
-            acc = new_bank((7 + i) % 8)
-            cols = slice(n0, n0 + width)
-            for g in range(PASSES):
-                multiply(acc[:, 0:width], "wc", n0, width, last, g)
-            nc.vector.tensor_tensor(out=c[:, cols], in0=acc[:, 0:width], in1=bias_c[:, cols], op=ADD)
-            nc.scalar.activation(c[:, cols], c[:, cols], SIGMOID)
-            nc.scalar.activation(c[:, cols], c[:, cols], TANH)
-            nc.vector.tensor_tensor(out=c[:, cols], in0=c[:, cols], in1=o[:, cols], op=MULT)
-            nc.sync.dma_start(out=out_rows[P * last : P * (last + 1), cols], in_=c[:, cols])
+                    multiply(acc[:, 0:width], "wo", n0, width, t, g)
+                finish(t, acc, c, o, n0, width)

@@ -105,8 +105,9 @@ def tile_mdlstm_kernel(
         x0_wc_scales(0, 2)
         load_codes("x0", x_words, BLOCK // 2, BLOCK // 2, 0, 1)
         x0_wc_codes(1, 2)
-        x0_wc_codes(2, 4)
         x0_wc_scales(2, 6)
+        x0_wc_codes(2, 3)
+        x0_wc_codes(3, 4)
         x0_wc_codes(4, 8)
         x0_wc_scales(6, 11)
         x0_wc_codes(8, 12)

from contextlib import ExitStack

import concourse.mybir as mybir

ROWS, K, N = 3072, 8192, 512

F32 = mybir.dt.float32
BF16 = mybir.dt.bfloat16
I32 = mybir.dt.int32
U8 = mybir.dt.uint8
FP4X4 = mybir.dt.float4_e2m1fn_x4
ADD = mybir.AluOpType.add
MULT = mybir.AluOpType.mult
SIGMOID = mybir.ActivationFunctionType.Sigmoid
TANH = mybir.ActivationFunctionType.Tanh

P = 128
PASSES = K // 512
BLOCK = 1024
TILES = BLOCK // P
BLOCKS = ROWS // BLOCK
TAIL = 4
WARM = 7

FLOPS = 2 * ROWS * K * (2 * N)
BYTES = ROWS * K // 2 + ROWS * K // 32 + 2 * (N * K // 2 + N * K // 32) + 2 * 2 * N + 4 * ROWS * N


def tile_mdlstm_kernel(
    tc, x_words, x_scales, wf, uf, biasf, wi, ui, biasi, wo_words, wo_scales, uo, biaso, wc_words, wc_scales, uc, biasc, out
):
    nc = tc.nc
    out_rows = out.rearrange("i j b n -> (i j b) n")

    with ExitStack() as ctx:
        keep = ctx.enter_context(tc.tile_pool(name="keep", bufs=1))
        acts = ctx.enter_context(tc.tile_pool(name="acts", bufs=4))
        psum = ctx.enter_context(tc.psum_pool(name="psum", bufs=1))
        ctx.enter_context(tc.manual_schedule())

        codes = {}
        planes = {}

        def new_planes(name, cols, g0, g1):
            tile = keep.tile([P, g1 - g0, cols], U8, name="%s_planes_%d" % (name, g0), align_bytes=256)
            nc.vector.memset(tile[:].bitcast(I32), 0)
            for g in range(g0, g1):
                planes[name, g] = tile[:, g - g0, :]
            return tile

        def load_scales(tile, scales, c0, cols, g0, g1):
            for q in range(4):
                nc.sync.dma_start(
                    out=tile[32 * q : 32 * q + 4, :, :].bitcast(I32),
                    in_=scales[g0:g1, 4 * q : 4 * q + 4, c0 : c0 + cols].rearrange("g r n -> r g n").bitcast(I32),
                )

        def load_codes(name, words, c0, cols, g0, g1):
            tile = keep.tile([P, g1 - g0, 2 * cols], U8, name="%s_codes_%d_%d" % (name, g0, c0), align_bytes=256)
            nc.sync.dma_start(
                out=tile[:].bitcast(I32),
                in_=words[g0:g1, :, 2 * c0 : 2 * (c0 + cols)].rearrange("g p n -> p g n").bitcast(I32),
            )
            for g in range(g0, g1):
                for col in range(c0, c0 + cols, P):
                    codes[name[0:1], g, col] = tile[:, g - g0, 2 * (col - c0) : 2 * (col - c0 + P)]
                codes[name, g] = tile[:, g - g0, :]

        def multiply(acc, w, w0, width, t, g):
            b, m0 = "x%d" % (t // TILES), P * (t % TILES)
            nc.tensor.matmul_mx(
                out=acc,
                lhsT=codes["x", g, P * t].bitcast(FP4X4),
                lhsT_scale=planes[b, g][:, m0 : m0 + P],
                rhs=codes[w, g][:, 2 * w0 : 2 * (w0 + width)].bitcast(FP4X4),
                rhs_scale=planes[w, g][:, w0 : w0 + width],
                start=(g == 0),
                stop=(g == PASSES - 1),
            )

        def new_bank(i):
            return psum.tile([P, N], F32, name="bank%d" % i)

        scale_runs = [(0, 2), (2, 6), (6, 11), (11, 16)]
        tiles0 = {}
        warm = keep.tile([P, N], BF16)
        nc.gpsimd.memset(warm[:], 0.0)
        for g0, g1 in scale_runs:
            tiles0["x0", g0] = new_planes("x0", BLOCK, g0, g1)
            tiles0["wc", g0] = new_planes("wc", N, g0, g1)
        wo_planes = new_planes("wo", N, 0, PASSES)
        x1_planes = new_planes("x1", BLOCK, 0, PASSES)
        x2_planes = new_planes("x2", BLOCK, 0, PASSES)

        def x0_wc_codes(g0, g1):
            load_codes("x0", x_words, 0, BLOCK, g0, g1)
            load_codes("wc", wc_words, 0, N, g0, g1)

        def x0_wc_scales(g0, g1):
            load_scales(tiles0["x0", g0], x_scales, 0, BLOCK, g0, g1)
            load_scales(tiles0["wc", g0], wc_scales, 0, N, g0, g1)

        load_codes("x0", x_words, 0, BLOCK // 2, 0, 1)
        load_codes("wc", wc_words, 0, N, 0, 1)
        x0_wc_scales(0, 2)
        load_codes("x0", x_words, BLOCK // 2, BLOCK // 2, 0, 1)
        x0_wc_codes(1, 2)
        x0_wc_scales(2, 6)
        x0_wc_codes(2, 3)
        x0_wc_codes(3, 4)
        x0_wc_codes(4, 8)
        x0_wc_scales(6, 11)
        x0_wc_codes(8, 12)
        x0_wc_scales(11, 16)
        x0_wc_codes(12, 16)

        bias_c = keep.tile([P, N], BF16)
        nc.sync.dma_start(out=bias_c[:], in_=biasc.partition_broadcast(P))
        bias_o = keep.tile([P, N], BF16)
        nc.sync.dma_start(out=bias_o[:], in_=biaso.partition_broadcast(P))

        load_codes("wo", wo_words, 0, N, 0, 8)
        load_codes("wo", wo_words, 0, N, 8, 16)
        load_scales(wo_planes, wo_scales, 0, N, 0, PASSES)

        def load_block(i, x_planes):
            for g0 in range(0, PASSES, 4):
                load_codes("x%d" % i, x_words, i * BLOCK, BLOCK, g0, g0 + 4)
            load_scales(x_planes, x_scales, i * BLOCK, BLOCK, 0, PASSES)

        load_block(1, x1_planes)

        scrap = new_bank(7)
        for i in range(WARM):
            nc.tensor.matmul(scrap[:], warm[:, 0:P], warm[:], start=True, stop=True)

        def cell(acc):
            c = acts.tile([P, N], F32, name="c", bufs=9)
            nc.vector.tensor_tensor(out=c[:], in0=acc[:], in1=bias_c[:], op=ADD)
            nc.scalar.activation(c[:], c[:], SIGMOID)
            nc.scalar.activation(c[:], c[:], TANH)
            return c

        def finish(t, acc, c, o, n0, width):
            cols = slice(n0, n0 + width)
            nc.vector.tensor_tensor(out=o[:, cols], in0=acc[:, 0:width], in1=bias_o[:, cols], op=ADD)
            nc.scalar.activation(o[:, cols], o[:, cols], SIGMOID)
            nc.vector.tensor_tensor(out=o[:, cols], in0=o[:, cols], in1=c[:, cols], op=MULT)
            nc.sync.dma_start(out=out_rows[P * t : P * (t + 1), cols], in_=o[:, cols])

        banks = [new_bank(t) for t in range(TILES)]
        for g in range(PASSES - TAIL):
            for t in range(TILES):
                multiply(banks[t][:], "wc", 0, N, t, g)
        cells = []
        for t in range(TILES):
            for g in range(PASSES - TAIL, PASSES):
                multiply(banks[t][:], "wc", 0, N, t, g)
            cells.append(cell(banks[t]))

        for t in range(TILES):
            acc = new_bank(t)
            for g in range(PASSES):
                multiply(acc[:], "wo", 0, N, t, g)
            o = acts.tile([P, N], F32, name="o", bufs=4)
            finish(t, acc, cells[t], o, 0, N)

        load_block(2, x2_planes)

        last = BLOCKS * TILES - 1
        for t in range(TILES, last + 1):
            acc = new_bank(2 * t % 8)
            for g in range(PASSES):
                multiply(acc[:], "wc", 0, N, t, g)
            c = cell(acc)
            o = acts.tile([P, N], F32, name="o", bufs=4)
            pieces = [(0, N)] if t < last else [(0, 256), (256, 128), (384, 128)]
            for i, (n0, width) in enumerate(pieces):
                acc = new_bank((2 * t + 1 + i) % 8)
                for g in range(PASSES):
                    multiply(acc[:, 0:width], "wo", n0, width, t, g)
                finish(t, acc, c, o, n0, width)
